import numpy as np
import ml_dtypes

BF16 = ml_dtypes.bfloat16


def bf(x):
    return np.asarray(x, np.float32).astype(BF16)


def f32(x):
    return np.asarray(x, np.float32)


def f64(x):
    return np.asarray(x).astype(np.float64)


def striped(idx):
    return np.tile(idx.reshape(-1, 16).T, (8, 1))


U, S, RL, H, K, N = 128, 512, 4, 256, 8, 2048
K_GAIN = 4.0


def setup_inputs():
    return {"table": bf(np.random.standard_normal((U, S))), "rel_w": bf(np.random.standard_normal((RL, U, U)) / np.sqrt(U)), "k_w": bf(K_GAIN * np.random.standard_normal((U, U)) / np.sqrt(U)), "v_w": bf(np.random.standard_normal((U, U)) / np.sqrt(U)), "offs": striped(np.concatenate([np.random.permutation(S)[:H] for _ in range(K)]))}


def reference(table, rel_w, k_w, v_w, offs):
    idx = offs[:16].T.reshape(-1)
    x = f64(table)[:, idx]
    nb = np.concatenate([f64(rel_w)[r].T @ x[:, r * S:(r + 1) * S] for r in range(RL)], axis=1)
    keys = f64(k_w).T @ nb / np.sqrt(U)
    vals = f64(v_w).T @ nb
    return np.concatenate([keys, vals], axis=0)

@@ -1,0 +1,60 @@
+import math
+
+import concourse.mybir as mybir
+
+BF16, F32, U16 = mybir.dt.bfloat16, mybir.dt.float32, mybir.dt.uint16
+COPY = mybir.ActivationFunctionType.Copy
+
+U = 128
+S = 512
+RL = 4
+N = RL * S
+OFFS_COLS = S // 16
+
+FLOPS = 3 * 2 * U * U * N
+
+
+def tile_spatiallayer_kernel(tc, table, rel_w, k_w, v_w, offs, out):
+    nc = tc.nc
+    with (
+        tc.tile_pool(name="held", bufs=1) as held,
+        tc.tile_pool(name="work", bufs=RL) as work,
+        tc.psum_pool(name="nb_banks", bufs=RL) as nb_banks,
+        tc.psum_pool(name="out_banks", bufs=2) as out_banks,
+    ):
+        offsets = held.tile([U, N // 16], U16, name="offsets")
+        nc.sync.dma_start(offsets[:], offs)
+        table_sb = held.tile([U, S], BF16, name="table_sb")
+        nc.scalar.dma_start(table_sb[:], table)
+        rel_sb = held.tile([U, RL, U], BF16, name="rel_sb")
+        nc.sync.dma_start(rel_sb[:], rel_w.rearrange("r u h -> u r h"))
+        k_sb = held.tile([U, U], BF16, name="k_sb")
+        nc.scalar.dma_start(k_sb[:], k_w)
+        v_sb = held.tile([U, U], BF16, name="v_sb")
+        nc.scalar.dma_start(v_sb[:], v_w)
+
+        nb_ps = [nb_banks.tile([U, S], F32, name="nb_ps") for r in range(RL)]
+        for r in range(RL):
+            looked_up = table_sb[:].indirect(offsets[:, r * OFFS_COLS : (r + 1) * OFFS_COLS])
+            nc.tensor.matmul(nb_ps[r][:], rel_sb[:, r, :], looked_up, start=True, stop=True)
+
+        for r in range(RL):
+            columns = slice(r * S, (r + 1) * S)
+
+            nb = work.tile([U, S], BF16, name="nb")
+            if r % 2 == 0:
+                nc.vector.tensor_copy(nb[:], nb_ps[r][:])
+            else:
+                nc.scalar.copy(nb[:], nb_ps[r][:])
+
+            keys_ps = out_banks.tile([U, S], F32, name="keys_ps")
+            nc.tensor.matmul(keys_ps[:], k_sb[:], nb[:], start=True, stop=True)
+            keys = work.tile([U, S], F32, name="keys")
+            nc.scalar.activation(keys[:], keys_ps[:], COPY, scale=1.0 / math.sqrt(U))
+            nc.sync.dma_start(out[0:U, columns], keys[:])
+
+            vals_ps = out_banks.tile([U, S], F32, name="vals_ps")
+            nc.tensor.matmul(vals_ps[:], v_sb[:], nb[:], start=True, stop=True)
+            vals = work.tile([U, S], F32, name="vals")
+            nc.vector.tensor_copy(vals[:], vals_ps[:])
+            nc.sync.dma_start(out[U : 2 * U, columns], vals[:])

@@ -11,6 +11,8 @@ RL = 4
 N = RL * S
 OFFS_COLS = S // 16
 
+WARM_UPS = 4
+
 FLOPS = 3 * 2 * U * U * N
 
 
@@ -34,6 +36,12 @@ def tile_spatiallayer_kernel(tc, table, rel_w, k_w, v_w, offs, out):
         nc.scalar.dma_start(v_sb[:], v_w)
 
         nb_ps = [nb_banks.tile([U, S], F32, name="nb_ps") for r in range(RL)]
+
+        zeros = held.tile([U, S], BF16, name="zeros")
+        nc.vector.memset(zeros[:], 0.0)
+        for i in range(WARM_UPS):
+            nc.tensor.matmul(nb_ps[RL - 1][:], zeros[:, 0:U], zeros[:], start=True, stop=True)
+
         for r in range(RL):
             looked_up = table_sb[:].indirect(offsets[:, r * OFFS_COLS : (r + 1) * OFFS_COLS])
             nc.tensor.matmul(nb_ps[r][:], rel_sb[:, r, :], looked_up, start=True, stop=True)

@@ -11,8 +11,6 @@ RL = 4
 N = RL * S
 OFFS_COLS = S // 16
 
-WARM_UPS = 4
-
 FLOPS = 3 * 2 * U * U * N
 
 
@@ -29,19 +27,15 @@ def tile_spatiallayer_kernel(tc, table, rel_w, k_w, v_w, offs, out):
         table_sb = held.tile([U, S], BF16, name="table_sb")
         nc.scalar.dma_start(table_sb[:], table)
         rel_sb = held.tile([U, RL, U], BF16, name="rel_sb")
-        nc.sync.dma_start(rel_sb[:], rel_w.rearrange("r u h -> u r h"))
+        for r in range(RL):
+            queue = nc.sync if r % 2 == 0 else nc.scalar
+            queue.dma_start(rel_sb[:, r, :], rel_w[r])
         k_sb = held.tile([U, U], BF16, name="k_sb")
-        nc.scalar.dma_start(k_sb[:], k_w)
+        nc.gpsimd.dma_start(k_sb[:], k_w)
         v_sb = held.tile([U, U], BF16, name="v_sb")
-        nc.scalar.dma_start(v_sb[:], v_w)
+        nc.gpsimd.dma_start(v_sb[:], v_w)
 
         nb_ps = [nb_banks.tile([U, S], F32, name="nb_ps") for r in range(RL)]
-
-        zeros = held.tile([U, S], BF16, name="zeros")
-        nc.vector.memset(zeros[:], 0.0)
-        for i in range(WARM_UPS):
-            nc.tensor.matmul(nb_ps[RL - 1][:], zeros[:, 0:U], zeros[:], start=True, stop=True)
-
         for r in range(RL):
             looked_up = table_sb[:].indirect(offsets[:, r * OFFS_COLS : (r + 1) * OFFS_COLS])
             nc.tensor.matmul(nb_ps[r][:], rel_sb[:, r, :], looked_up, start=True, stop=True)

@@ -44,10 +44,7 @@ def tile_spatiallayer_kernel(tc, table, rel_w, k_w, v_w, offs, out):
             columns = slice(r * S, (r + 1) * S)
 
             nb = work.tile([U, S], BF16, name="nb")
-            if r % 2 == 0:
-                nc.vector.tensor_copy(nb[:], nb_ps[r][:])
-            else:
-                nc.scalar.copy(nb[:], nb_ps[r][:])
+            nc.vector.tensor_copy(nb[:], nb_ps[r][:])
 
             keys_ps = out_banks.tile([U, S], F32, name="keys_ps")
             nc.tensor.matmul(keys_ps[:], k_sb[:], nb[:], start=True, stop=True)

@@ -40,20 +40,24 @@ def tile_spatiallayer_kernel(tc, table, rel_w, k_w, v_w, offs, out):
             looked_up = table_sb[:].indirect(offsets[:, r * OFFS_COLS : (r + 1) * OFFS_COLS])
             nc.tensor.matmul(nb_ps[r][:], rel_sb[:, r, :], looked_up, start=True, stop=True)
 
+        out_halves = out.rearrange("(half m) j -> m half j", half=2)
         for r in range(RL):
             columns = slice(r * S, (r + 1) * S)
 
             nb = work.tile([U, S], BF16, name="nb")
-            nc.vector.tensor_copy(nb[:], nb_ps[r][:])
+            if r % 2 == 0:
+                nc.vector.tensor_copy(nb[:], nb_ps[r][:])
+            else:
+                nc.scalar.copy(nb[:], nb_ps[r][:])
+
+            both = work.tile([U, 2, S], F32, name="both")
 
             keys_ps = out_banks.tile([U, S], F32, name="keys_ps")
             nc.tensor.matmul(keys_ps[:], k_sb[:], nb[:], start=True, stop=True)
-            keys = work.tile([U, S], F32, name="keys")
-            nc.scalar.activation(keys[:], keys_ps[:], COPY, scale=1.0 / math.sqrt(U))
-            nc.sync.dma_start(out[0:U, columns], keys[:])
+            nc.scalar.activation(both[:, 0, :], keys_ps[:], COPY, scale=1.0 / math.sqrt(U))
 
             vals_ps = out_banks.tile([U, S], F32, name="vals_ps")
             nc.tensor.matmul(vals_ps[:], v_sb[:], nb[:], start=True, stop=True)
-            vals = work.tile([U, S], F32, name="vals")
-            nc.vector.tensor_copy(vals[:], vals_ps[:])
-            nc.sync.dma_start(out[U : 2 * U, columns], vals[:])
+            nc.vector.tensor_copy(both[:, 1, :], vals_ps[:])
+
+            nc.sync.dma_start(out_halves[:, :, columns], both[:])

@@ -40,7 +40,6 @@ def tile_spatiallayer_kernel(tc, table, rel_w, k_w, v_w, offs, out):
             looked_up = table_sb[:].indirect(offsets[:, r * OFFS_COLS : (r + 1) * OFFS_COLS])
             nc.tensor.matmul(nb_ps[r][:], rel_sb[:, r, :], looked_up, start=True, stop=True)
 
-        out_halves = out.rearrange("(half m) j -> m half j", half=2)
         for r in range(RL):
             columns = slice(r * S, (r + 1) * S)
 
@@ -50,14 +49,14 @@ def tile_spatiallayer_kernel(tc, table, rel_w, k_w, v_w, offs, out):
             else:
                 nc.scalar.copy(nb[:], nb_ps[r][:])
 
-            both = work.tile([U, 2, S], F32, name="both")
-
             keys_ps = out_banks.tile([U, S], F32, name="keys_ps")
             nc.tensor.matmul(keys_ps[:], k_sb[:], nb[:], start=True, stop=True)
-            nc.scalar.activation(both[:, 0, :], keys_ps[:], COPY, scale=1.0 / math.sqrt(U))
+            keys = work.tile([U, S], F32, name="keys")
+            nc.scalar.activation(keys[:], keys_ps[:], COPY, scale=1.0 / math.sqrt(U))
+            nc.scalar.dma_start(out[0:U, columns], keys[:])
 
             vals_ps = out_banks.tile([U, S], F32, name="vals_ps")
             nc.tensor.matmul(vals_ps[:], v_sb[:], nb[:], start=True, stop=True)
-            nc.vector.tensor_copy(both[:, 1, :], vals_ps[:])
-
-            nc.sync.dma_start(out_halves[:, :, columns], both[:])
+            vals = work.tile([U, S], F32, name="vals")
+            nc.vector.tensor_copy(vals[:], vals_ps[:])
+            nc.sync.dma_start(out[U : 2 * U, columns], vals[:])

@@ -59,4 +59,5 @@ def tile_spatiallayer_kernel(tc, table, rel_w, k_w, v_w, offs, out):
             nc.tensor.matmul(vals_ps[:], v_sb[:], nb[:], start=True, stop=True)
             vals = work.tile([U, S], F32, name="vals")
             nc.vector.tensor_copy(vals[:], vals_ps[:])
-            nc.sync.dma_start(out[U : 2 * U, columns], vals[:])
+            queue = nc.gpsimd if r % 2 == 0 else nc.sync
+            queue.dma_start(out[U : 2 * U, columns], vals[:])

@@ -31,9 +31,9 @@ def tile_spatiallayer_kernel(tc, table, rel_w, k_w, v_w, offs, out):
             queue = nc.sync if r % 2 == 0 else nc.scalar
             queue.dma_start(rel_sb[:, r, :], rel_w[r])
         k_sb = held.tile([U, U], BF16, name="k_sb")
-        nc.gpsimd.dma_start(k_sb[:], k_w)
+        nc.sync.dma_start(k_sb[:], k_w)
         v_sb = held.tile([U, U], BF16, name="v_sb")
-        nc.gpsimd.dma_start(v_sb[:], v_w)
+        nc.scalar.dma_start(v_sb[:], v_w)
 
         nb_ps = [nb_banks.tile([U, S], F32, name="nb_ps") for r in range(RL)]
         for r in range(RL):
@@ -59,5 +59,4 @@ def tile_spatiallayer_kernel(tc, table, rel_w, k_w, v_w, offs, out):
             nc.tensor.matmul(vals_ps[:], v_sb[:], nb[:], start=True, stop=True)
             vals = work.tile([U, S], F32, name="vals")
             nc.vector.tensor_copy(vals[:], vals_ps[:])
-            queue = nc.gpsimd if r % 2 == 0 else nc.sync
-            queue.dma_start(out[U : 2 * U, columns], vals[:])
+            nc.sync.dma_start(out[U : 2 * U, columns], vals[:])

@@ -9,7 +9,11 @@ U = 128
 S = 512
 RL = 4
 N = RL * S
-OFFS_COLS = S // 16
+PIECE = 256
+PIECES = N // PIECE
+PER_REL = S // PIECE
+OFFS_COLS = PIECE // 16
+BANKS = 8
 
 FLOPS = 3 * 2 * U * U * N
 
@@ -18,9 +22,9 @@ def tile_spatiallayer_kernel(tc, table, rel_w, k_w, v_w, offs, out):
     nc = tc.nc
     with (
         tc.tile_pool(name="held", bufs=1) as held,
-        tc.tile_pool(name="work", bufs=RL) as work,
-        tc.psum_pool(name="nb_banks", bufs=RL) as nb_banks,
-        tc.psum_pool(name="out_banks", bufs=2) as out_banks,
+        tc.tile_pool(name="rounded", bufs=PIECES) as rounded,
+        tc.tile_pool(name="staged", bufs=RL) as staged,
+        tc.psum_pool(name="banks", bufs=BANKS) as banks,
     ):
         offsets = held.tile([U, N // 16], U16, name="offsets")
         nc.sync.dma_start(offsets[:], offs)
@@ -35,28 +39,32 @@ def tile_spatiallayer_kernel(tc, table, rel_w, k_w, v_w, offs, out):
         v_sb = held.tile([U, U], BF16, name="v_sb")
         nc.scalar.dma_start(v_sb[:], v_w)
 
-        nb_ps = [nb_banks.tile([U, S], F32, name="nb_ps") for r in range(RL)]
-        for r in range(RL):
-            looked_up = table_sb[:].indirect(offsets[:, r * OFFS_COLS : (r + 1) * OFFS_COLS])
-            nc.tensor.matmul(nb_ps[r][:], rel_sb[:, r, :], looked_up, start=True, stop=True)
+        nb_ps = [banks.tile([U, PIECE], F32, name="bank") for t in range(PIECES)]
+        for t in range(PIECES):
+            looked_up = table_sb[:].indirect(offsets[:, t * OFFS_COLS : (t + 1) * OFFS_COLS])
+            nc.tensor.matmul(nb_ps[t][:], rel_sb[:, t // PER_REL, :], looked_up, start=True, stop=True)
 
-        for r in range(RL):
-            columns = slice(r * S, (r + 1) * S)
-
-            nb = work.tile([U, S], BF16, name="nb")
-            if r % 2 == 0:
-                nc.vector.tensor_copy(nb[:], nb_ps[r][:])
+        nb = [rounded.tile([U, PIECE], BF16, name="nb") for t in range(PIECES)]
+        for t in range(PIECES):
+            if t % 2 == 0:
+                nc.scalar.copy(nb[t][:], nb_ps[t][:])
             else:
-                nc.scalar.copy(nb[:], nb_ps[r][:])
+                nc.vector.tensor_copy(nb[t][:], nb_ps[t][:])
 
-            keys_ps = out_banks.tile([U, S], F32, name="keys_ps")
-            nc.tensor.matmul(keys_ps[:], k_sb[:], nb[:], start=True, stop=True)
-            keys = work.tile([U, S], F32, name="keys")
-            nc.scalar.activation(keys[:], keys_ps[:], COPY, scale=1.0 / math.sqrt(U))
+        for r in range(RL):
+            keys = staged.tile([U, S], F32, name="keys")
+            vals = staged.tile([U, S], F32, name="vals")
+            for t in range(r * PER_REL, (r + 1) * PER_REL):
+                part = slice((t % PER_REL) * PIECE, (t % PER_REL + 1) * PIECE)
+
+                keys_ps = banks.tile([U, PIECE], F32, name="bank")
+                nc.tensor.matmul(keys_ps[:], k_sb[:], nb[t][:], start=True, stop=True)
+                nc.scalar.activation(keys[:, part], keys_ps[:], COPY, scale=1.0 / math.sqrt(U))
+
+                vals_ps = banks.tile([U, PIECE], F32, name="bank")
+                nc.tensor.matmul(vals_ps[:], v_sb[:], nb[t][:], start=True, stop=True)
+                nc.vector.tensor_copy(vals[:, part], vals_ps[:])
+
+            columns = slice(r * S, (r + 1) * S)
             nc.scalar.dma_start(out[0:U, columns], keys[:])
-
-            vals_ps = out_banks.tile([U, S], F32, name="vals_ps")
-            nc.tensor.matmul(vals_ps[:], v_sb[:], nb[:], start=True, stop=True)
-            vals = work.tile([U, S], F32, name="vals")
-            nc.vector.tensor_copy(vals[:], vals_ps[:])
             nc.sync.dma_start(out[U : 2 * U, columns], vals[:])

@@ -14,6 +14,8 @@ PIECES = N // PIECE
 PER_REL = S // PIECE
 OFFS_COLS = PIECE // 16
 BANKS = 8
+FIRST_RUN = 3 * PER_REL
+HALF = PIECE // 2
 
 FLOPS = 3 * 2 * U * U * N
 
@@ -39,32 +41,35 @@ def tile_spatiallayer_kernel(tc, table, rel_w, k_w, v_w, offs, out):
         v_sb = held.tile([U, U], BF16, name="v_sb")
         nc.scalar.dma_start(v_sb[:], v_w)
 
-        nb_ps = [banks.tile([U, PIECE], F32, name="bank") for t in range(PIECES)]
-        for t in range(PIECES):
-            looked_up = table_sb[:].indirect(offsets[:, t * OFFS_COLS : (t + 1) * OFFS_COLS])
-            nc.tensor.matmul(nb_ps[t][:], rel_sb[:, t // PER_REL, :], looked_up, start=True, stop=True)
+        def project(weights, nb_piece):
+            product = banks.tile([U, PIECE], F32, name="bank")
+            for half in (slice(0, HALF), slice(HALF, PIECE)):
+                nc.tensor.matmul(product[:, half], weights[:], nb_piece[:, half], start=True, stop=True)
+            return product
 
-        nb = [rounded.tile([U, PIECE], BF16, name="nb") for t in range(PIECES)]
-        for t in range(PIECES):
-            if t % 2 == 0:
-                nc.scalar.copy(nb[t][:], nb_ps[t][:])
-            else:
-                nc.vector.tensor_copy(nb[t][:], nb_ps[t][:])
+        for run in (range(0, FIRST_RUN), range(FIRST_RUN, PIECES)):
+            nb_ps = {t: banks.tile([U, PIECE], F32, name="bank") for t in run}
+            for t in run:
+                looked_up = table_sb[:].indirect(offsets[:, t * OFFS_COLS : (t + 1) * OFFS_COLS])
+                nc.tensor.matmul(nb_ps[t][:], rel_sb[:, t // PER_REL, :], looked_up, start=True, stop=True)
 
-        for r in range(RL):
-            keys = staged.tile([U, S], F32, name="keys")
-            vals = staged.tile([U, S], F32, name="vals")
-            for t in range(r * PER_REL, (r + 1) * PER_REL):
-                part = slice((t % PER_REL) * PIECE, (t % PER_REL + 1) * PIECE)
+            nb = {t: rounded.tile([U, PIECE], BF16, name="nb") for t in run}
+            for t in run:
+                if t % 2 == 0:
+                    nc.scalar.copy(nb[t][:], nb_ps[t][:])
+                else:
+                    nc.vector.tensor_copy(nb[t][:], nb_ps[t][:])
 
-                keys_ps = banks.tile([U, PIECE], F32, name="bank")
-                nc.tensor.matmul(keys_ps[:], k_sb[:], nb[t][:], start=True, stop=True)
-                nc.scalar.activation(keys[:, part], keys_ps[:], COPY, scale=1.0 / math.sqrt(U))
+            for r in range(run.start // PER_REL, run.stop // PER_REL):
+                keys = staged.tile([U, S], F32, name="keys")
+                vals = staged.tile([U, S], F32, name="vals")
+                for t in range(r * PER_REL, (r + 1) * PER_REL):
+                    part = slice((t % PER_REL) * PIECE, (t % PER_REL + 1) * PIECE)
+                    keys_ps = project(k_sb, nb[t])
+                    nc.scalar.activation(keys[:, part], keys_ps[:], COPY, scale=1.0 / math.sqrt(U))
+                    vals_ps = project(v_sb, nb[t])
+                    nc.vector.tensor_copy(vals[:, part], vals_ps[:])
 
-                vals_ps = banks.tile([U, PIECE], F32, name="bank")
-                nc.tensor.matmul(vals_ps[:], v_sb[:], nb[t][:], start=True, stop=True)
-                nc.vector.tensor_copy(vals[:, part], vals_ps[:])
-
-            columns = slice(r * S, (r + 1) * S)
-            nc.scalar.dma_start(out[0:U, columns], keys[:])
-            nc.sync.dma_start(out[U : 2 * U, columns], vals[:])
+                columns = slice(r * S, (r + 1) * S)
+                nc.scalar.dma_start(out[0:U, columns], keys[:])
+                nc.sync.dma_start(out[U : 2 * U, columns], vals[:])

@@ -24,8 +24,6 @@ def tile_spatiallayer_kernel(tc, table, rel_w, k_w, v_w, offs, out):
     nc = tc.nc
     with (
         tc.tile_pool(name="held", bufs=1) as held,
-        tc.tile_pool(name="rounded", bufs=PIECES) as rounded,
-        tc.tile_pool(name="staged", bufs=RL) as staged,
         tc.psum_pool(name="banks", bufs=BANKS) as banks,
     ):
         offsets = held.tile([U, N // 16], U16, name="offsets")
@@ -41,35 +39,46 @@ def tile_spatiallayer_kernel(tc, table, rel_w, k_w, v_w, offs, out):
         v_sb = held.tile([U, U], BF16, name="v_sb")
         nc.scalar.dma_start(v_sb[:], v_w)
 
-        def project(weights, nb_piece):
-            product = banks.tile([U, PIECE], F32, name="bank")
-            for half in (slice(0, HALF), slice(HALF, PIECE)):
-                nc.tensor.matmul(product[:, half], weights[:], nb_piece[:, half], start=True, stop=True)
-            return product
+        nb = held.tile([U, N], BF16, name="nb")
+        staged = held.tile([U, 2, N], F32, name="staged")
 
-        for run in (range(0, FIRST_RUN), range(FIRST_RUN, PIECES)):
-            nb_ps = {t: banks.tile([U, PIECE], F32, name="bank") for t in run}
-            for t in run:
+        def columns(pieces):
+            return slice(pieces.start * PIECE, pieces.stop * PIECE)
+
+        def look_up(pieces):
+            nb_ps = {t: banks.tile([U, PIECE], F32, name="bank") for t in pieces}
+            for t in pieces:
                 looked_up = table_sb[:].indirect(offsets[:, t * OFFS_COLS : (t + 1) * OFFS_COLS])
                 nc.tensor.matmul(nb_ps[t][:], rel_sb[:, t // PER_REL, :], looked_up, start=True, stop=True)
+            for t in pieces:
+                move_out(nb[:, columns(range(t, t + 1))], nb_ps[t], 1.0, t)
 
-            nb = {t: rounded.tile([U, PIECE], BF16, name="nb") for t in run}
-            for t in run:
-                if t % 2 == 0:
-                    nc.scalar.copy(nb[t][:], nb_ps[t][:])
-                else:
-                    nc.vector.tensor_copy(nb[t][:], nb_ps[t][:])
+        def move_out(target, bank, scale, t):
+            if t % 2 == 0:
+                nc.scalar.activation(target, bank[:], COPY, scale=scale)
+            else:
+                nc.vector.tensor_scalar_mul(target, bank[:], scale)
 
-            for r in range(run.start // PER_REL, run.stop // PER_REL):
-                keys = staged.tile([U, S], F32, name="keys")
-                vals = staged.tile([U, S], F32, name="vals")
-                for t in range(r * PER_REL, (r + 1) * PER_REL):
-                    part = slice((t % PER_REL) * PIECE, (t % PER_REL + 1) * PIECE)
-                    keys_ps = project(k_sb, nb[t])
-                    nc.scalar.activation(keys[:, part], keys_ps[:], COPY, scale=1.0 / math.sqrt(U))
-                    vals_ps = project(v_sb, nb[t])
-                    nc.vector.tensor_copy(vals[:, part], vals_ps[:])
+        def project_and_store(which, weights, scale, pieces, queue):
+            for t in pieces:
+                product = banks.tile([U, PIECE], F32, name="bank")
+                for first in (t * PIECE, t * PIECE + HALF):
+                    nc.tensor.matmul(
+                        product[:, first - t * PIECE : first - t * PIECE + HALF],
+                        weights[:],
+                        nb[:, first : first + HALF],
+                        start=True,
+                        stop=True,
+                    )
+                move_out(staged[:, which, columns(range(t, t + 1))], product, scale, t)
+            queue.dma_start(out[which * U : (which + 1) * U, columns(pieces)], staged[:, which, columns(pieces)])
 
-                columns = slice(r * S, (r + 1) * S)
-                nc.scalar.dma_start(out[0:U, columns], keys[:])
-                nc.sync.dma_start(out[U : 2 * U, columns], vals[:])
+        k_scale = 1.0 / math.sqrt(U)
+
+        look_up(range(0, FIRST_RUN))
+        project_and_store(0, k_sb, k_scale, range(0, PER_REL), nc.sync)
+        project_and_store(0, k_sb, k_scale, range(PER_REL, FIRST_RUN), nc.scalar)
+        project_and_store(1, v_sb, 1.0, range(0, FIRST_RUN), nc.sync)
+        look_up(range(FIRST_RUN, PIECES))
+        project_and_store(0, k_sb, k_scale, range(FIRST_RUN, PIECES), nc.scalar)
+        project_and_store(1, v_sb, 1.0, range(FIRST_RUN, PIECES), nc.sync)

@@ -59,14 +59,14 @@ def tile_spatiallayer_kernel(tc, table, rel_w, k_w, v_w, offs, out):
             else:
                 nc.vector.tensor_scalar_mul(target, bank[:], scale)
 
-        def project_and_store(which, weights, scale, pieces, queue):
+        def project_and_store(which, weights, scale, pieces, width, queue):
             for t in pieces:
                 product = banks.tile([U, PIECE], F32, name="bank")
-                for first in (t * PIECE, t * PIECE + HALF):
+                for first in range(0, PIECE, width):
                     nc.tensor.matmul(
-                        product[:, first - t * PIECE : first - t * PIECE + HALF],
+                        product[:, first : first + width],
                         weights[:],
-                        nb[:, first : first + HALF],
+                        nb[:, t * PIECE + first : t * PIECE + first + width],
                         start=True,
                         stop=True,
                     )
@@ -76,9 +76,9 @@ def tile_spatiallayer_kernel(tc, table, rel_w, k_w, v_w, offs, out):
         k_scale = 1.0 / math.sqrt(U)
 
         look_up(range(0, FIRST_RUN))
-        project_and_store(0, k_sb, k_scale, range(0, PER_REL), nc.sync)
-        project_and_store(0, k_sb, k_scale, range(PER_REL, FIRST_RUN), nc.scalar)
-        project_and_store(1, v_sb, 1.0, range(0, FIRST_RUN), nc.sync)
+        project_and_store(0, k_sb, k_scale, range(0, PER_REL), HALF, nc.sync)
+        project_and_store(0, k_sb, k_scale, range(PER_REL, FIRST_RUN), HALF, nc.scalar)
+        project_and_store(1, v_sb, 1.0, range(0, FIRST_RUN), HALF, nc.sync)
         look_up(range(FIRST_RUN, PIECES))
-        project_and_store(0, k_sb, k_scale, range(FIRST_RUN, PIECES), nc.scalar)
-        project_and_store(1, v_sb, 1.0, range(FIRST_RUN, PIECES), nc.sync)
+        project_and_store(0, k_sb, k_scale, range(FIRST_RUN, PIECES), PIECE, nc.scalar)
+        project_and_store(1, v_sb, 1.0, range(FIRST_RUN, PIECES), PIECE, nc.sync)

@@ -55,9 +55,9 @@ def tile_spatiallayer_kernel(tc, table, rel_w, k_w, v_w, offs, out):
 
         def move_out(target, bank, scale, t):
             if t % 2 == 0:
-                nc.scalar.activation(target, bank[:], COPY, scale=scale)
-            else:
                 nc.vector.tensor_scalar_mul(target, bank[:], scale)
+            else:
+                nc.scalar.activation(target, bank[:], COPY, scale=scale)
 
         def project_and_store(which, weights, scale, pieces, width, queue):
             for t in pieces:
@@ -75,10 +75,9 @@ def tile_spatiallayer_kernel(tc, table, rel_w, k_w, v_w, offs, out):
 
         k_scale = 1.0 / math.sqrt(U)
 
-        look_up(range(0, FIRST_RUN))
-        project_and_store(0, k_sb, k_scale, range(0, PER_REL), HALF, nc.sync)
-        project_and_store(0, k_sb, k_scale, range(PER_REL, FIRST_RUN), HALF, nc.scalar)
-        project_and_store(1, v_sb, 1.0, range(0, FIRST_RUN), HALF, nc.sync)
-        look_up(range(FIRST_RUN, PIECES))
-        project_and_store(0, k_sb, k_scale, range(FIRST_RUN, PIECES), PIECE, nc.scalar)
-        project_and_store(1, v_sb, 1.0, range(FIRST_RUN, PIECES), PIECE, nc.sync)
+        for run, width in ((range(0, FIRST_RUN), HALF), (range(FIRST_RUN, PIECES), PIECE)):
+            look_up(run)
+            for first in range(run.start, run.stop, PER_REL):
+                relation = range(first, first + PER_REL)
+                project_and_store(0, k_sb, k_scale, relation, width, nc.scalar)
+                project_and_store(1, v_sb, 1.0, relation, width, nc.sync)

@@ -14,8 +14,8 @@ PIECES = N // PIECE
 PER_REL = S // PIECE
 OFFS_COLS = PIECE // 16
 BANKS = 8
-FIRST_RUN = 3 * PER_REL
-HALF = PIECE // 2
+FIRST_RUN = 2 * PER_REL
+QUARTER = PIECE // 4
 
 FLOPS = 3 * 2 * U * U * N
 
@@ -75,7 +75,7 @@ def tile_spatiallayer_kernel(tc, table, rel_w, k_w, v_w, offs, out):
 
         k_scale = 1.0 / math.sqrt(U)
 
-        for run, width in ((range(0, FIRST_RUN), HALF), (range(FIRST_RUN, PIECES), PIECE)):
+        for run, width in ((range(0, FIRST_RUN), QUARTER), (range(FIRST_RUN, PIECES), PIECE)):
             look_up(run)
             for first in range(run.start, run.stop, PER_REL):
                 relation = range(first, first + PER_REL)

@@ -15,7 +15,8 @@ PER_REL = S // PIECE
 OFFS_COLS = PIECE // 16
 BANKS = 8
 FIRST_RUN = 2 * PER_REL
-QUARTER = PIECE // 4
+THIRDS = (96, 80, 80)
+WHOLE = (PIECE,)
 
 FLOPS = 3 * 2 * U * U * N
 
@@ -59,10 +60,11 @@ def tile_spatiallayer_kernel(tc, table, rel_w, k_w, v_w, offs, out):
             else:
                 nc.scalar.activation(target, bank[:], COPY, scale=scale)
 
-        def project_and_store(which, weights, scale, pieces, width, queue):
+        def project_and_store(which, weights, scale, pieces, widths, queue):
             for t in pieces:
                 product = banks.tile([U, PIECE], F32, name="bank")
-                for first in range(0, PIECE, width):
+                first = 0
+                for width in widths:
                     nc.tensor.matmul(
                         product[:, first : first + width],
                         weights[:],
@@ -70,14 +72,15 @@ def tile_spatiallayer_kernel(tc, table, rel_w, k_w, v_w, offs, out):
                         start=True,
                         stop=True,
                     )
+                    first += width
                 move_out(staged[:, which, columns(range(t, t + 1))], product, scale, t)
             queue.dma_start(out[which * U : (which + 1) * U, columns(pieces)], staged[:, which, columns(pieces)])
 
         k_scale = 1.0 / math.sqrt(U)
 
-        for run, width in ((range(0, FIRST_RUN), QUARTER), (range(FIRST_RUN, PIECES), PIECE)):
+        for run, widths in ((range(0, FIRST_RUN), THIRDS), (range(FIRST_RUN, PIECES), WHOLE)):
             look_up(run)
             for first in range(run.start, run.stop, PER_REL):
                 relation = range(first, first + PER_REL)
-                project_and_store(0, k_sb, k_scale, relation, width, nc.scalar)
-                project_and_store(1, v_sb, 1.0, relation, width, nc.sync)
+                project_and_store(0, k_sb, k_scale, relation, widths, nc.scalar)
+                project_and_store(1, v_sb, 1.0, relation, widths, nc.sync)

@@ -32,13 +32,14 @@ def tile_spatiallayer_kernel(tc, table, rel_w, k_w, v_w, offs, out):
         table_sb = held.tile([U, S], BF16, name="table_sb")
         nc.scalar.dma_start(table_sb[:], table)
         rel_sb = held.tile([U, RL, U], BF16, name="rel_sb")
-        for r in range(RL):
-            queue = nc.sync if r % 2 == 0 else nc.scalar
-            queue.dma_start(rel_sb[:, r, :], rel_w[r])
         k_sb = held.tile([U, U], BF16, name="k_sb")
-        nc.sync.dma_start(k_sb[:], k_w)
         v_sb = held.tile([U, U], BF16, name="v_sb")
+        nc.sync.dma_start(rel_sb[:, 0, :], rel_w[0])
+        nc.scalar.dma_start(rel_sb[:, 1, :], rel_w[1])
+        nc.sync.dma_start(k_sb[:], k_w)
         nc.scalar.dma_start(v_sb[:], v_w)
+        nc.sync.dma_start(rel_sb[:, 2, :], rel_w[2])
+        nc.scalar.dma_start(rel_sb[:, 3, :], rel_w[3])
 
         nb = held.tile([U, N], BF16, name="nb")
         staged = held.tile([U, 2, N], F32, name="staged")

import math

import concourse.mybir as mybir

BF16, F32, U16 = mybir.dt.bfloat16, mybir.dt.float32, mybir.dt.uint16
COPY = mybir.ActivationFunctionType.Copy

U = 128
S = 512
RL = 4
N = RL * S
PIECE = 256
PIECES = N // PIECE
PER_REL = S // PIECE
OFFS_COLS = PIECE // 16
BANKS = 8
FIRST_RUN = 2 * PER_REL
THIRDS = (96, 80, 80)
WHOLE = (PIECE,)

FLOPS = 3 * 2 * U * U * N


def tile_spatiallayer_kernel(tc, table, rel_w, k_w, v_w, offs, out):
    nc = tc.nc
    with (
        tc.tile_pool(name="held", bufs=1) as held,
        tc.psum_pool(name="banks", bufs=BANKS) as banks,
    ):
        offsets = held.tile([U, N // 16], U16, name="offsets")
        nc.sync.dma_start(offsets[:], offs)
        table_sb = held.tile([U, S], BF16, name="table_sb")
        nc.scalar.dma_start(table_sb[:], table)
        rel_sb = held.tile([U, RL, U], BF16, name="rel_sb")
        k_sb = held.tile([U, U], BF16, name="k_sb")
        v_sb = held.tile([U, U], BF16, name="v_sb")
        nc.sync.dma_start(rel_sb[:, 0, :], rel_w[0])
        nc.scalar.dma_start(rel_sb[:, 1, :], rel_w[1])
        nc.sync.dma_start(k_sb[:], k_w)
        nc.scalar.dma_start(v_sb[:], v_w)
        nc.sync.dma_start(rel_sb[:, 2, :], rel_w[2])
        nc.scalar.dma_start(rel_sb[:, 3, :], rel_w[3])

        nb = held.tile([U, N], BF16, name="nb")
        staged = held.tile([U, 2, N], F32, name="staged")

        def columns(pieces):
            return slice(pieces.start * PIECE, pieces.stop * PIECE)

        def look_up(pieces):
            nb_ps = {t: banks.tile([U, PIECE], F32, name="bank") for t in pieces}
            for t in pieces:
                looked_up = table_sb[:].indirect(offsets[:, t * OFFS_COLS : (t + 1) * OFFS_COLS])
                nc.tensor.matmul(nb_ps[t][:], rel_sb[:, t // PER_REL, :], looked_up, start=True, stop=True)
            for t in pieces:
                move_out(nb[:, columns(range(t, t + 1))], nb_ps[t], 1.0, t)

        def move_out(target, bank, scale, t):
            if t % 2 == 0:
                nc.vector.tensor_scalar_mul(target, bank[:], scale)
            else:
                nc.scalar.activation(target, bank[:], COPY, scale=scale)

        def project_and_store(which, weights, scale, pieces, widths, queue):
            for t in pieces:
                product = banks.tile([U, PIECE], F32, name="bank")
                first = 0
                for width in widths:
                    nc.tensor.matmul(
                        product[:, first : first + width],
                        weights[:],
                        nb[:, t * PIECE + first : t * PIECE + first + width],
                        start=True,
                        stop=True,
                    )
                    first += width
                move_out(staged[:, which, columns(range(t, t + 1))], product, scale, t)
            queue.dma_start(out[which * U : (which + 1) * U, columns(pieces)], staged[:, which, columns(pieces)])

        k_scale = 1.0 / math.sqrt(U)

        for run, widths in ((range(0, FIRST_RUN), THIRDS), (range(FIRST_RUN, PIECES), WHOLE)):
            look_up(run)
            for first in range(run.start, run.stop, PER_REL):
                relation = range(first, first + PER_REL)
                project_and_store(0, k_sb, k_scale, relation, widths, nc.scalar)
                project_and_store(1, v_sb, 1.0, relation, widths, nc.sync)
